import numpy as np
import ml_dtypes


def mxq(x, axis, fmt="e4m3"):
    dtype, down = {"e4m3": (ml_dtypes.float8_e4m3fn, 7), "e5m2": (ml_dtypes.float8_e5m2, 14)}[fmt]
    v = np.moveaxis(np.asarray(x, np.float32).astype(ml_dtypes.bfloat16).astype(np.float64), axis, -1)
    blocks = v.reshape(v.shape[:-1] + (-1, 32))
    amax = np.abs(blocks).max(-1, keepdims=True)
    byte = np.maximum(np.where(amax > 0, np.frexp(amax)[1] - 1 + 127, 0) - down, 1)
    scale = np.exp2(byte - 127.0)
    codes = (blocks / scale).astype(np.float32).astype(dtype).astype(np.float64)
    return np.moveaxis((codes * scale).reshape(v.shape), -1, axis)


WIDE = False


def mx_kscale(k):
    if not WIDE:
        return np.ones(k)
    levels = np.array([10, -10, 5, -5, 0])
    if k % 512:
        return np.exp2(np.random.permutation(np.resize(levels, k // 32))).repeat(32)
    a = np.empty((k // 512, 16))
    for p in range(k // 512):
        a[p, :8] = np.random.permutation(np.resize(levels, 8))
        for g in range(8):
            far = levels[np.abs(levels - a[p, g]) >= 10]
            a[p, g + 8] = far[np.random.randint(len(far))]
    return np.exp2(a.ravel()).repeat(32)


BF16 = ml_dtypes.bfloat16


def bf(x):
    return np.asarray(x, np.float32).astype(BF16)


def f64(x):
    return np.asarray(x).astype(np.float64)


B, D0, D1, D2, D3, D4 = 8192, 512, 512, 512, 1024, 256
DENSITY = 0.02


def setup_inputs():
    s, t = mx_kscale(D0), mx_kscale(D1)
    bound0 = np.sqrt(3.0 / (DENSITY * D0))
    bound1 = np.sqrt(6.0 / (DENSITY * D1))
    return {"x": bf(np.random.standard_normal((B, D0)) * s),
            "W0": bf(np.random.uniform(-bound0, bound0, (D1, D0)) / s[None, :] * t[:, None]),
            "b0": bf(np.random.standard_normal(D1) * 0.3 * t),
            "m0": bf(np.random.uniform(size=(D1, D0)) < DENSITY),
            "W1": bf(np.random.uniform(-bound1, bound1, (D2, D1)) / t[None, :]),
            "b1": bf(np.random.standard_normal(D2) * 0.3),
            "m1": bf(np.random.uniform(size=(D2, D1)) < DENSITY)}


def reference(x, W0, b0, m0, W1, b1, m1):
    h = f64(x).reshape(x.shape[0], -1)
    w0 = f64(W0) * f64(m0)
    pre0 = (mxq(h, 1, "e4m3") @ mxq(w0, 1, "e4m3").T) + f64(b0)
    h0 = np.maximum(pre0, 0.0)
    w1 = f64(W1) * f64(m1)
    pre1 = (mxq(h0, 1, "e4m3") @ mxq(w1, 1, "e4m3").T) + f64(b1)
    return np.maximum(pre1, 0.0)

@@ -1,0 +1,232 @@
+from contextlib import ExitStack
+
+import concourse.mybir as mybir
+from concourse.masks import make_identity
+
+F32 = mybir.dt.float32
+BF16 = mybir.dt.bfloat16
+U32 = mybir.dt.uint32
+U8 = mybir.dt.uint8
+FP8X4 = mybir.dt.float8_e4m3fn_x4
+ALU = mybir.AluOpType
+ACT = mybir.ActivationFunctionType
+
+P = 128
+PACK = 4
+WIDTH = P * PACK
+TOKENS = 8192
+GROUPS = TOKENS // WIDTH
+HALF = WIDTH // 2
+FLOAT32_MAX = 3.4028234663852886e38
+
+FLOPS = 2 * 2 * TOKENS * WIDTH * WIDTH
+
+
+def tile_patchedsparsenetwork_pa_t_kernel(tc, x, W0, b0, m0, W1, b1, m1, out):
+    nc = tc.nc
+    x_groups = x.rearrange("(g p r) k -> g p (r k)", p=P, r=PACK)
+    out_groups = out.rearrange("(g p r) d -> g p r d", p=P, r=PACK)
+
+    with ExitStack() as ctx:
+        consts = ctx.enter_context(tc.tile_pool(name="consts", bufs=1))
+        x_pool = ctx.enter_context(tc.tile_pool(name="x_pool", bufs=GROUPS))
+        grouped_pool = ctx.enter_context(tc.tile_pool(name="grouped_pool", bufs=3))
+        mx_pool = ctx.enter_context(tc.tile_pool(name="mx_pool", bufs=3))
+        out_pool = ctx.enter_context(tc.tile_pool(name="out_pool", bufs=4))
+        psum_scalar = ctx.enter_context(tc.psum_pool(name="psum_scalar", bufs=4))
+        psum_vector = ctx.enter_context(tc.psum_pool(name="psum_vector", bufs=4))
+        ctx.enter_context(tc.manual_schedule())
+
+        x_rows = {}
+
+        def load_x(g):
+            x_rows[g] = x_pool.tile([P, PACK * WIDTH], BF16, name="x_rows", tag="x_rows")
+            nc.sync.dma_start(out=x_rows[g][:], in_=x_groups[g])
+
+        def load_weight_and_mask(W, m, rows_of_partition, name):
+            raw = consts.tile([P, PACK * WIDTH], BF16, name=name + "_raw")
+            mask = consts.tile([P, PACK * WIDTH], BF16, name=name + "_mask")
+            for half in range(2):
+                for tile_, source in ((raw, W), (mask, m)):
+                    nc.sync.dma_start(
+                        out=tile_[:, half * PACK * HALF : (half + 1) * PACK * HALF].rearrange(
+                            "m (b k) -> m b k", k=WIDTH
+                        ),
+                        in_=source.rearrange(rows_of_partition, m=P)[:, half * PACK // 2 : (half + 1) * PACK // 2, :],
+                    )
+            return raw, mask
+
+        b0_bf = consts.tile([P, PACK], BF16)
+        b1_bf = consts.tile([P, WIDTH], BF16)
+
+        load_x(0)
+        w0_raw, m0_raw = load_weight_and_mask(W0, m0, "(m t) k -> m t k", "w0")
+        load_x(1)
+        nc.sync.dma_start(out=b0_bf[:], in_=b0.rearrange("(m t) -> m t", t=PACK))
+        w1_raw, m1_raw = load_weight_and_mask(W1, m1, "(j m) k -> m j k", "w1")
+        load_x(2)
+        nc.sync.dma_start(out=b1_bf[:], in_=b1.partition_broadcast(P))
+        for g in range(3, GROUPS):
+            load_x(g)
+
+        ident = consts.tile([P, P], F32)
+        make_identity(nc, ident[:])
+
+        def rows_onto_partitions(words, grouped):
+            grouped_words = grouped[:].bitcast(F32).rearrange("q (c u) -> q c u", u=2)
+            for half in range(2):
+                bank = psum_scalar.tile([P, 2, HALF], F32, name="bank", tag="bank")
+                for b in range(2):
+                    for u in range(2):
+                        nc.tensor.transpose(bank[:, u, b * P : (b + 1) * P], words[:, 2 * half + b, u, :], ident[:])
+                nc.scalar.copy(
+                    out=grouped_words[:, half * HALF : (half + 1) * HALF, :], in_=bank[:].rearrange("q u c -> q c u")
+                )
+
+        def quantise_halves(grouped, codes, scales):
+            for half in range(2):
+                nc.vector.quantize_mx(
+                    out=codes[:, half * HALF : (half + 1) * HALF].bitcast(FP8X4),
+                    scales=scales[:, half * HALF : (half + 1) * HALF],
+                    in_=grouped[:, half * PACK * HALF : (half + 1) * PACK * HALF],
+                )
+
+        def mask_weight(raw, mask, name):
+            masked = consts.tile([P, PACK * WIDTH], BF16, name=name + "_masked")
+            for half in range(2):
+                cols = slice(half * PACK * HALF, (half + 1) * PACK * HALF)
+                nc.vector.tensor_tensor(out=masked[:, cols], in0=raw[:, cols], in1=mask[:, cols], op=ALU.mult)
+            return masked
+
+        def transpose_weight(masked, word_order, name):
+            grouped = consts.tile([P, PACK * WIDTH], BF16, name=name + "_grouped", align_bytes=64)
+            rows_onto_partitions(masked[:].bitcast(F32).rearrange(word_order, b=PACK, u=2), grouped)
+            return grouped
+
+        def quantise_weight(grouped, name):
+            codes = consts.tile([P, WIDTH], U32, name=name + "_codes", align_bytes=64)
+            scales = consts.tile([P, WIDTH], U8, name=name + "_scales", align_bytes=64)
+            quantise_halves(grouped, codes, scales)
+            return codes, scales
+
+        def mx_tiles(name):
+            codes = mx_pool.tile([P, WIDTH], U32, name=name + "_codes", tag=name + "_codes", align_bytes=64)
+            scales = mx_pool.tile([P, WIDTH], U8, name=name + "_scales", tag=name + "_scales", align_bytes=64)
+            return codes, scales
+
+        x_grouped = {}
+        x_mx = {}
+        h_planes = {}
+        h_grouped = {}
+        h_mx = {}
+        results = {}
+
+        def transpose_x(g):
+            x_grouped[g] = grouped_pool.tile(
+                [P, PACK * WIDTH], BF16, name="x_grouped", tag="x_grouped", align_bytes=64
+            )
+            rows_onto_partitions(
+                x_rows[g][:].bitcast(F32).rearrange("p (b q u) -> p b u q", b=PACK, u=2), x_grouped[g]
+            )
+
+        def quantise_x(g):
+            x_mx[g] = mx_tiles("x")
+            codes, scales = x_mx[g]
+            nc.vector.quantize_mx(out=codes[:].bitcast(FP8X4), scales=scales[:], in_=x_grouped[g][:])
+
+        def layer1(g):
+            codes, scales = x_mx[g]
+            h_planes[g] = grouped_pool.tile([P, PACK, WIDTH], BF16, name="h_planes", tag="h_planes")
+            for t in range(PACK):
+                acc = psum_scalar.tile([P, WIDTH], F32, name="acc1", tag="bank")
+                nc.tensor.matmul_mx(
+                    out=acc[:],
+                    lhsT=w0_codes[:, t * P : (t + 1) * P].bitcast(FP8X4),
+                    lhsT_scale=w0_scales[:, t * P : (t + 1) * P],
+                    rhs=codes[:].bitcast(FP8X4),
+                    rhs_scale=scales[:],
+                    start=True,
+                    stop=True,
+                )
+                nc.scalar.activation(
+                    out=h_planes[g][:, t, :], in_=acc[:], func=ACT.Relu, bias=b0_f32[:, t : t + 1], scale=1.0
+                )
+
+        def regroup_h(g):
+            h_grouped[g] = grouped_pool.tile(
+                [P, PACK * WIDTH], BF16, name="h_grouped", tag="h_grouped", align_bytes=64
+            )
+            nc.vector.tensor_copy(
+                out=h_grouped[g][:].rearrange("p (c i t) -> p c t i", i=4, t=PACK),
+                in_=h_planes[g][:].rearrange("p t (c i) -> p c t i", i=4),
+            )
+
+        def quantise_h(g):
+            h_mx[g] = mx_tiles("h")
+            quantise_halves(h_grouped[g], h_mx[g][0], h_mx[g][1])
+
+        def layer2(g):
+            codes, scales = h_mx[g]
+            results[g] = out_pool.tile([P, PACK, WIDTH], F32, name="result", tag="result")
+            for r in range(PACK):
+                acc = psum_vector.tile([P, WIDTH], F32, name="acc2", tag="acc2")
+                nc.tensor.matmul_mx(
+                    out=acc[:],
+                    lhsT=codes[:, r * P : (r + 1) * P].bitcast(FP8X4),
+                    lhsT_scale=scales[:, r * P : (r + 1) * P],
+                    rhs=w1_codes[:].bitcast(FP8X4),
+                    rhs_scale=w1_scales[:],
+                    start=True,
+                    stop=True,
+                )
+                nc.vector.tensor_tensor(out=results[g][:, r, :], in0=acc[:], in1=b1_f32[:], op=ALU.add)
+
+        def relu_first_half(g):
+            for r in range(PACK // 2):
+                nc.gpsimd.tensor_scalar(
+                    out=results[g][:, r, :],
+                    in0=results[g][:, r, :],
+                    scalar1=FLOAT32_MAX,
+                    scalar2=0.0,
+                    op0=ALU.min,
+                    op1=ALU.max,
+                )
+            nc.sync.dma_start(out=out_groups[g][:, : PACK // 2, :], in_=results[g][:, : PACK // 2, :])
+
+        def relu_second_half(g):
+            for r in range(PACK // 2, PACK):
+                nc.scalar.activation(out=results[g][:, r, :], in_=results[g][:, r, :], func=ACT.Relu)
+            nc.sync.dma_start(out=out_groups[g][:, PACK // 2 :, :], in_=results[g][:, PACK // 2 :, :])
+
+        transpose_x(0)
+        w0_masked = mask_weight(w0_raw, m0_raw, "w0")
+        quantise_x(0)
+        w0_grouped = transpose_weight(w0_masked, "m (b q u) -> m b u q", "w0")
+        w0_codes, w0_scales = quantise_weight(w0_grouped, "w0")
+        b0_f32 = consts.tile([P, PACK], F32)
+        nc.vector.tensor_copy(out=b0_f32[:], in_=b0_bf[:])
+        transpose_x(1)
+        layer1(0)
+        w1_masked = mask_weight(w1_raw, m1_raw, "w1")
+        quantise_x(1)
+        w1_grouped = transpose_weight(w1_masked, "m (b q u) -> m b u q", "w1")
+        transpose_x(2)
+        layer1(1)
+        transpose_x(3)
+        regroup_h(0)
+        w1_codes, w1_scales = quantise_weight(w1_grouped, "w1")
+        b1_f32 = consts.tile([P, WIDTH], F32)
+        nc.vector.tensor_copy(out=b1_f32[:], in_=b1_bf[:])
+        for g in range(GROUPS):
+            quantise_h(g)
+            if g + 2 < GROUPS:
+                quantise_x(g + 2)
+            if g + 1 < GROUPS:
+                regroup_h(g + 1)
+            layer2(g)
+            relu_first_half(g)
+            if g + 2 < GROUPS:
+                layer1(g + 2)
+            if g + 4 < GROUPS:
+                transpose_x(g + 4)
+            relu_second_half(g)

@@ -17,6 +17,7 @@ WIDTH = P * PACK
 TOKENS = 8192
 GROUPS = TOKENS // WIDTH
 HALF = WIDTH // 2
+SCALAR_TOKENS = 128
 FLOAT32_MAX = 3.4028234663852886e38
 
 FLOPS = 2 * 2 * TOKENS * WIDTH * WIDTH
@@ -152,14 +153,24 @@ def tile_patchedsparsenetwork_pa_t_kernel(tc, x, W0, b0, m0, W1, b1, m1, out):
                     out=h_planes[g][:, t, :], in_=acc[:], func=ACT.Relu, bias=b0_f32[:, t : t + 1], scale=1.0
                 )
 
-        def regroup_h(g):
+        def regroup_views(g, tokens):
+            grouped = h_grouped[g][:, tokens.start * PACK : tokens.stop * PACK]
+            planes = h_planes[g][:, :, tokens]
+            return (
+                grouped.rearrange("p (c i t) -> p c t i", i=4, t=PACK),
+                planes.rearrange("p t (c i) -> p c t i", i=4),
+            )
+
+        def regroup_h_on_scalar(g):
             h_grouped[g] = grouped_pool.tile(
                 [P, PACK * WIDTH], BF16, name="h_grouped", tag="h_grouped", align_bytes=64
             )
-            nc.vector.tensor_copy(
-                out=h_grouped[g][:].rearrange("p (c i t) -> p c t i", i=4, t=PACK),
-                in_=h_planes[g][:].rearrange("p t (c i) -> p c t i", i=4),
-            )
+            grouped, planes = regroup_views(g, slice(WIDTH - SCALAR_TOKENS, WIDTH))
+            nc.scalar.copy(out=grouped, in_=planes)
+
+        def regroup_h_on_vector(g):
+            grouped, planes = regroup_views(g, slice(0, WIDTH - SCALAR_TOKENS))
+            nc.vector.tensor_copy(out=grouped, in_=planes)
 
         def quantise_h(g):
             h_mx[g] = mx_tiles("h")
@@ -181,8 +192,8 @@ def tile_patchedsparsenetwork_pa_t_kernel(tc, x, W0, b0, m0, W1, b1, m1, out):
                 )
                 nc.vector.tensor_tensor(out=results[g][:, r, :], in0=acc[:], in1=b1_f32[:], op=ALU.add)
 
-        def relu_first_half(g):
-            for r in range(PACK // 2):
+        def relu_on_gpsimd(g):
+            for r in range(PACK - 1):
                 nc.gpsimd.tensor_scalar(
                     out=results[g][:, r, :],
                     in0=results[g][:, r, :],
@@ -193,8 +204,8 @@ def tile_patchedsparsenetwork_pa_t_kernel(tc, x, W0, b0, m0, W1, b1, m1, out):
                 )
             nc.sync.dma_start(out=out_groups[g][:, : PACK // 2, :], in_=results[g][:, : PACK // 2, :])
 
-        def relu_second_half(g):
-            for r in range(PACK // 2, PACK):
+        def relu_on_scalar(g):
+            for r in range(PACK - 1, PACK):
                 nc.scalar.activation(out=results[g][:, r, :], in_=results[g][:, r, :], func=ACT.Relu)
             nc.sync.dma_start(out=out_groups[g][:, PACK // 2 :, :], in_=results[g][:, PACK // 2 :, :])
 
@@ -212,8 +223,10 @@ def tile_patchedsparsenetwork_pa_t_kernel(tc, x, W0, b0, m0, W1, b1, m1, out):
         w1_grouped = transpose_weight(w1_masked, "m (b q u) -> m b u q", "w1")
         transpose_x(2)
         layer1(1)
+        regroup_h_on_scalar(0)
         transpose_x(3)
-        regroup_h(0)
+        regroup_h_on_vector(0)
+        regroup_h_on_scalar(1)
         w1_codes, w1_scales = quantise_weight(w1_grouped, "w1")
         b1_f32 = consts.tile([P, WIDTH], F32)
         nc.vector.tensor_copy(out=b1_f32[:], in_=b1_bf[:])
@@ -222,11 +235,13 @@ def tile_patchedsparsenetwork_pa_t_kernel(tc, x, W0, b0, m0, W1, b1, m1, out):
             if g + 2 < GROUPS:
                 quantise_x(g + 2)
             if g + 1 < GROUPS:
-                regroup_h(g + 1)
+                regroup_h_on_vector(g + 1)
             layer2(g)
-            relu_first_half(g)
+            relu_on_gpsimd(g)
             if g + 2 < GROUPS:
                 layer1(g + 2)
             if g + 4 < GROUPS:
                 transpose_x(g + 4)
-            relu_second_half(g)
+            if g + 2 < GROUPS:
+                regroup_h_on_scalar(g + 2)
+            relu_on_scalar(g)

@@ -17,7 +17,9 @@ WIDTH = P * PACK
 TOKENS = 8192
 GROUPS = TOKENS // WIDTH
 HALF = WIDTH // 2
-SCALAR_TOKENS = 128
+SCALAR_TOKENS = {g: 128 for g in range(GROUPS)}
+SCALAR_TOKENS[GROUPS - 1] = 384
+SCALAR_TOKENS[0] = SCALAR_TOKENS[1] = 0
 FLOAT32_MAX = 3.4028234663852886e38
 
 FLOPS = 2 * 2 * TOKENS * WIDTH * WIDTH
@@ -73,14 +75,14 @@ def tile_patchedsparsenetwork_pa_t_kernel(tc, x, W0, b0, m0, W1, b1, m1, out):
         ident = consts.tile([P, P], F32)
         make_identity(nc, ident[:])
 
-        def rows_onto_partitions(words, grouped):
+        def rows_onto_partitions(words, grouped, copies=(nc.scalar.copy, nc.scalar.copy)):
             grouped_words = grouped[:].bitcast(F32).rearrange("q (c u) -> q c u", u=2)
             for half in range(2):
                 bank = psum_scalar.tile([P, 2, HALF], F32, name="bank", tag="bank")
                 for b in range(2):
                     for u in range(2):
                         nc.tensor.transpose(bank[:, u, b * P : (b + 1) * P], words[:, 2 * half + b, u, :], ident[:])
-                nc.scalar.copy(
+                copies[half](
                     out=grouped_words[:, half * HALF : (half + 1) * HALF, :], in_=bank[:].rearrange("q u c -> q c u")
                 )
 
@@ -122,12 +124,12 @@ def tile_patchedsparsenetwork_pa_t_kernel(tc, x, W0, b0, m0, W1, b1, m1, out):
         h_mx = {}
         results = {}
 
-        def transpose_x(g):
+        def transpose_x(g, copies=(nc.scalar.copy, nc.scalar.copy)):
             x_grouped[g] = grouped_pool.tile(
                 [P, PACK * WIDTH], BF16, name="x_grouped", tag="x_grouped", align_bytes=64
             )
             rows_onto_partitions(
-                x_rows[g][:].bitcast(F32).rearrange("p (b q u) -> p b u q", b=PACK, u=2), x_grouped[g]
+                x_rows[g][:].bitcast(F32).rearrange("p (b q u) -> p b u q", b=PACK, u=2), x_grouped[g], copies
             )
 
         def quantise_x(g):
@@ -161,15 +163,17 @@ def tile_patchedsparsenetwork_pa_t_kernel(tc, x, W0, b0, m0, W1, b1, m1, out):
                 planes.rearrange("p t (c i) -> p c t i", i=4),
             )
 
-        def regroup_h_on_scalar(g):
+        def new_h_grouped(g):
             h_grouped[g] = grouped_pool.tile(
                 [P, PACK * WIDTH], BF16, name="h_grouped", tag="h_grouped", align_bytes=64
             )
-            grouped, planes = regroup_views(g, slice(WIDTH - SCALAR_TOKENS, WIDTH))
+
+        def regroup_h_on_scalar(g):
+            grouped, planes = regroup_views(g, slice(WIDTH - SCALAR_TOKENS[g], WIDTH))
             nc.scalar.copy(out=grouped, in_=planes)
 
         def regroup_h_on_vector(g):
-            grouped, planes = regroup_views(g, slice(0, WIDTH - SCALAR_TOKENS))
+            grouped, planes = regroup_views(g, slice(0, WIDTH - SCALAR_TOKENS[g]))
             nc.vector.tensor_copy(out=grouped, in_=planes)
 
         def quantise_h(g):
@@ -190,47 +194,63 @@ def tile_patchedsparsenetwork_pa_t_kernel(tc, x, W0, b0, m0, W1, b1, m1, out):
                     start=True,
                     stop=True,
                 )
-                nc.vector.tensor_tensor(out=results[g][:, r, :], in0=acc[:], in1=b1_f32[:], op=ALU.add)
+                nc.vector.tensor_tensor(out=results[g][:, r, :], in0=acc[:], in1=b1_bf[:], op=ALU.add)
+
+        def relu_gpsimd(block):
+            nc.gpsimd.tensor_scalar(
+                out=block, in0=block, scalar1=FLOAT32_MAX, scalar2=0.0, op0=ALU.min, op1=ALU.max
+            )
+
+        def relu_scalar(block):
+            nc.scalar.activation(out=block, in_=block, func=ACT.Relu)
+
+        def relu_vector(block):
+            nc.vector.tensor_scalar(out=block, in0=block, scalar1=0.0, scalar2=None, op0=ALU.max)
 
         def relu_on_gpsimd(g):
             for r in range(PACK - 1):
-                nc.gpsimd.tensor_scalar(
-                    out=results[g][:, r, :],
-                    in0=results[g][:, r, :],
-                    scalar1=FLOAT32_MAX,
-                    scalar2=0.0,
-                    op0=ALU.min,
-                    op1=ALU.max,
-                )
+                relu_gpsimd(results[g][:, r, :])
             nc.sync.dma_start(out=out_groups[g][:, : PACK // 2, :], in_=results[g][:, : PACK // 2, :])
 
         def relu_on_scalar(g):
-            for r in range(PACK - 1, PACK):
-                nc.scalar.activation(out=results[g][:, r, :], in_=results[g][:, r, :], func=ACT.Relu)
+            relu_scalar(results[g][:, PACK - 1, :])
             nc.sync.dma_start(out=out_groups[g][:, PACK // 2 :, :], in_=results[g][:, PACK // 2 :, :])
 
+        def relu_and_store_block(g, r, relu):
+            relu(results[g][:, r, :])
+            nc.sync.dma_start(out=out_groups[g][:, r, :], in_=results[g][:, r, :])
+
+        b0_f32 = consts.tile([P, PACK], F32)
         transpose_x(0)
         w0_masked = mask_weight(w0_raw, m0_raw, "w0")
         quantise_x(0)
         w0_grouped = transpose_weight(w0_masked, "m (b q u) -> m b u q", "w0")
         w0_codes, w0_scales = quantise_weight(w0_grouped, "w0")
-        b0_f32 = consts.tile([P, PACK], F32)
-        nc.vector.tensor_copy(out=b0_f32[:], in_=b0_bf[:])
-        transpose_x(1)
+        transpose_x(1, (nc.scalar.copy, nc.vector.tensor_copy))
+        nc.scalar.copy(out=b0_f32[:], in_=b0_bf[:])
         layer1(0)
         w1_masked = mask_weight(w1_raw, m1_raw, "w1")
         quantise_x(1)
         w1_grouped = transpose_weight(w1_masked, "m (b q u) -> m b u q", "w1")
         transpose_x(2)
-        layer1(1)
-        regroup_h_on_scalar(0)
-        transpose_x(3)
+        new_h_grouped(0)
         regroup_h_on_vector(0)
-        regroup_h_on_scalar(1)
+        layer1(1)
         w1_codes, w1_scales = quantise_weight(w1_grouped, "w1")
-        b1_f32 = consts.tile([P, WIDTH], F32)
-        nc.vector.tensor_copy(out=b1_f32[:], in_=b1_bf[:])
-        for g in range(GROUPS):
+        quantise_h(0)
+        quantise_x(2)
+        layer2(0)
+        relu_on_gpsimd(0)
+        new_h_grouped(1)
+        regroup_h_on_vector(1)
+        transpose_x(3)
+        layer1(2)
+        transpose_x(4)
+        new_h_grouped(2)
+        regroup_h_on_scalar(2)
+        relu_on_scalar(0)
+        last = GROUPS - 1
+        for g in range(1, last):
             quantise_h(g)
             if g + 2 < GROUPS:
                 quantise_x(g + 2)
@@ -243,5 +263,12 @@ def tile_patchedsparsenetwork_pa_t_kernel(tc, x, W0, b0, m0, W1, b1, m1, out):
             if g + 4 < GROUPS:
                 transpose_x(g + 4)
             if g + 2 < GROUPS:
+                new_h_grouped(g + 2)
                 regroup_h_on_scalar(g + 2)
             relu_on_scalar(g)
+        quantise_h(last)
+        layer2(last)
+        relu_and_store_block(last, 0, relu_gpsimd)
+        relu_and_store_block(last, 1, relu_scalar)
+        relu_and_store_block(last, 2, relu_scalar)
+        relu_and_store_block(last, 3, relu_vector)

@@ -44,7 +44,10 @@ def tile_patchedsparsenetwork_pa_t_kernel(tc, x, W0, b0, m0, W1, b1, m1, out):
 
         def load_x(g):
             x_rows[g] = x_pool.tile([P, PACK * WIDTH], BF16, name="x_rows", tag="x_rows")
-            nc.sync.dma_start(out=x_rows[g][:], in_=x_groups[g])
+            pieces = 2 if g == 0 else 1
+            for piece in range(pieces):
+                cols = slice(piece * PACK * WIDTH // pieces, (piece + 1) * PACK * WIDTH // pieces)
+                nc.sync.dma_start(out=x_rows[g][:, cols], in_=x_groups[g][:, cols])
 
         def load_weight_and_mask(W, m, rows_of_partition, name):
             raw = consts.tile([P, PACK * WIDTH], BF16, name=name + "_raw")
@@ -96,14 +99,19 @@ def tile_patchedsparsenetwork_pa_t_kernel(tc, x, W0, b0, m0, W1, b1, m1, out):
 
         def mask_weight(raw, mask, name):
             masked = consts.tile([P, PACK * WIDTH], BF16, name=name + "_masked")
-            for half in range(2):
-                cols = slice(half * PACK * HALF, (half + 1) * PACK * HALF)
-                nc.vector.tensor_tensor(out=masked[:, cols], in0=raw[:, cols], in1=mask[:, cols], op=ALU.mult)
+            for b in range(PACK):
+                cols = slice(b * WIDTH, (b + 1) * WIDTH)
+                nc.vector.tensor_tensor(
+                    out=masked[:, cols].rearrange("m (u q e) -> m u q e", u=2, e=2),
+                    in0=raw[:, cols].rearrange("m (q u e) -> m u q e", u=2, e=2),
+                    in1=mask[:, cols].rearrange("m (q u e) -> m u q e", u=2, e=2),
+                    op=ALU.mult,
+                )
             return masked
 
-        def transpose_weight(masked, word_order, name):
+        def transpose_weight(masked, name):
             grouped = consts.tile([P, PACK * WIDTH], BF16, name=name + "_grouped", align_bytes=64)
-            rows_onto_partitions(masked[:].bitcast(F32).rearrange(word_order, b=PACK, u=2), grouped)
+            rows_onto_partitions(masked[:].bitcast(F32).rearrange("m (b u q) -> m b u q", b=PACK, u=2), grouped)
             return grouped
 
         def quantise_weight(grouped, name):
@@ -224,14 +232,14 @@ def tile_patchedsparsenetwork_pa_t_kernel(tc, x, W0, b0, m0, W1, b1, m1, out):
         transpose_x(0)
         w0_masked = mask_weight(w0_raw, m0_raw, "w0")
         quantise_x(0)
-        w0_grouped = transpose_weight(w0_masked, "m (b q u) -> m b u q", "w0")
+        w0_grouped = transpose_weight(w0_masked, "w0")
         w0_codes, w0_scales = quantise_weight(w0_grouped, "w0")
         transpose_x(1, (nc.scalar.copy, nc.vector.tensor_copy))
         nc.scalar.copy(out=b0_f32[:], in_=b0_bf[:])
         layer1(0)
         w1_masked = mask_weight(w1_raw, m1_raw, "w1")
         quantise_x(1)
-        w1_grouped = transpose_weight(w1_masked, "m (b q u) -> m b u q", "w1")
+        w1_grouped = transpose_weight(w1_masked, "w1")
         transpose_x(2)
         new_h_grouped(0)
         regroup_h_on_vector(0)

@@ -17,6 +17,7 @@ WIDTH = P * PACK
 TOKENS = 8192
 GROUPS = TOKENS // WIDTH
 HALF = WIDTH // 2
+LINE = 8
 SCALAR_TOKENS = {g: 128 for g in range(GROUPS)}
 SCALAR_TOKENS[GROUPS - 1] = 384
 SCALAR_TOKENS[0] = SCALAR_TOKENS[1] = 0
@@ -127,7 +128,7 @@ def tile_patchedsparsenetwork_pa_t_kernel(tc, x, W0, b0, m0, W1, b1, m1, out):
 
         x_grouped = {}
         x_mx = {}
-        h_planes = {}
+        h_lines = {}
         h_grouped = {}
         h_mx = {}
         results = {}
@@ -147,7 +148,8 @@ def tile_patchedsparsenetwork_pa_t_kernel(tc, x, W0, b0, m0, W1, b1, m1, out):
 
         def layer1(g):
             codes, scales = x_mx[g]
-            h_planes[g] = grouped_pool.tile([P, PACK, WIDTH], BF16, name="h_planes", tag="h_planes")
+            h_lines[g] = grouped_pool.tile([P, PACK * WIDTH], BF16, name="h_lines", tag="h_lines", align_bytes=64)
+            lines = h_lines[g][:].rearrange("p (c t i) -> p c t i", i=LINE, t=PACK)
             for t in range(PACK):
                 acc = psum_scalar.tile([P, WIDTH], F32, name="acc1", tag="bank")
                 nc.tensor.matmul_mx(
@@ -160,15 +162,18 @@ def tile_patchedsparsenetwork_pa_t_kernel(tc, x, W0, b0, m0, W1, b1, m1, out):
                     stop=True,
                 )
                 nc.scalar.activation(
-                    out=h_planes[g][:, t, :], in_=acc[:], func=ACT.Relu, bias=b0_f32[:, t : t + 1], scale=1.0
+                    out=lines[:, :, t, :],
+                    in_=acc[:].rearrange("p (c i) -> p c i", i=LINE),
+                    func=ACT.Relu,
+                    bias=b0_f32[:, t : t + 1],
+                    scale=1.0,
                 )
 
         def regroup_views(g, tokens):
-            grouped = h_grouped[g][:, tokens.start * PACK : tokens.stop * PACK]
-            planes = h_planes[g][:, :, tokens]
+            elements = slice(tokens.start * PACK, tokens.stop * PACK)
             return (
-                grouped.rearrange("p (c i t) -> p c t i", i=4, t=PACK),
-                planes.rearrange("p t (c i) -> p c t i", i=4),
+                h_grouped[g][:, elements].rearrange("p (c i t) -> p c t i", i=LINE, t=PACK),
+                h_lines[g][:, elements].rearrange("p (c t i) -> p c t i", i=LINE, t=PACK),
             )
 
         def new_h_grouped(g):

@@ -147,27 +147,32 @@ def tile_patchedsparsenetwork_pa_t_kernel(tc, x, W0, b0, m0, W1, b1, m1, out):
             nc.vector.quantize_mx(out=codes[:].bitcast(FP8X4), scales=scales[:], in_=x_grouped[g][:])
 
         def layer1(g):
-            codes, scales = x_mx[g]
-            h_lines[g] = grouped_pool.tile([P, PACK * WIDTH], BF16, name="h_lines", tag="h_lines", align_bytes=64)
-            lines = h_lines[g][:].rearrange("p (c t i) -> p c t i", i=LINE, t=PACK)
+            new_h_lines(g)
             for t in range(PACK):
-                acc = psum_scalar.tile([P, WIDTH], F32, name="acc1", tag="bank")
-                nc.tensor.matmul_mx(
-                    out=acc[:],
-                    lhsT=w0_codes[:, t * P : (t + 1) * P].bitcast(FP8X4),
-                    lhsT_scale=w0_scales[:, t * P : (t + 1) * P],
-                    rhs=codes[:].bitcast(FP8X4),
-                    rhs_scale=scales[:],
-                    start=True,
-                    stop=True,
-                )
-                nc.scalar.activation(
-                    out=lines[:, :, t, :],
-                    in_=acc[:].rearrange("p (c i) -> p c i", i=LINE),
-                    func=ACT.Relu,
-                    bias=b0_f32[:, t : t + 1],
-                    scale=1.0,
-                )
+                layer1_plane(g, t)
+
+        def new_h_lines(g):
+            h_lines[g] = grouped_pool.tile([P, PACK * WIDTH], BF16, name="h_lines", tag="h_lines", align_bytes=64)
+
+        def layer1_plane(g, t):
+            codes, scales = x_mx[g]
+            acc = psum_scalar.tile([P, WIDTH], F32, name="acc1", tag="bank")
+            nc.tensor.matmul_mx(
+                out=acc[:],
+                lhsT=w0_codes[:, t * P : (t + 1) * P].bitcast(FP8X4),
+                lhsT_scale=w0_scales[:, t * P : (t + 1) * P],
+                rhs=codes[:].bitcast(FP8X4),
+                rhs_scale=scales[:],
+                start=True,
+                stop=True,
+            )
+            nc.scalar.activation(
+                out=h_lines[g][:].rearrange("p (c t i) -> p c t i", i=LINE, t=PACK)[:, :, t, :],
+                in_=acc[:].rearrange("p (c i) -> p c i", i=LINE),
+                func=ACT.Relu,
+                bias=b0_f32[:, t : t + 1],
+                scale=1.0,
+            )
 
         def regroup_views(g, tokens):
             elements = slice(tokens.start * PACK, tokens.stop * PACK)
@@ -194,20 +199,26 @@ def tile_patchedsparsenetwork_pa_t_kernel(tc, x, W0, b0, m0, W1, b1, m1, out):
             quantise_halves(h_grouped[g], h_mx[g][0], h_mx[g][1])
 
         def layer2(g):
-            codes, scales = h_mx[g]
-            results[g] = out_pool.tile([P, PACK, WIDTH], F32, name="result", tag="result")
+            new_results(g)
             for r in range(PACK):
-                acc = psum_vector.tile([P, WIDTH], F32, name="acc2", tag="acc2")
-                nc.tensor.matmul_mx(
-                    out=acc[:],
-                    lhsT=codes[:, r * P : (r + 1) * P].bitcast(FP8X4),
-                    lhsT_scale=scales[:, r * P : (r + 1) * P],
-                    rhs=w1_codes[:].bitcast(FP8X4),
-                    rhs_scale=w1_scales[:],
-                    start=True,
-                    stop=True,
-                )
-                nc.vector.tensor_tensor(out=results[g][:, r, :], in0=acc[:], in1=b1_bf[:], op=ALU.add)
+                layer2_block(g, r)
+
+        def new_results(g):
+            results[g] = out_pool.tile([P, PACK, WIDTH], F32, name="result", tag="result")
+
+        def layer2_block(g, r):
+            codes, scales = h_mx[g]
+            acc = psum_vector.tile([P, WIDTH], F32, name="acc2", tag="acc2")
+            nc.tensor.matmul_mx(
+                out=acc[:],
+                lhsT=codes[:, r * P : (r + 1) * P].bitcast(FP8X4),
+                lhsT_scale=scales[:, r * P : (r + 1) * P],
+                rhs=w1_codes[:].bitcast(FP8X4),
+                rhs_scale=w1_scales[:],
+                start=True,
+                stop=True,
+            )
+            nc.vector.tensor_tensor(out=results[g][:, r, :], in0=acc[:], in1=b1_bf[:], op=ALU.add)
 
         def relu_gpsimd(block):
             nc.gpsimd.tensor_scalar(
@@ -269,10 +280,16 @@ def tile_patchedsparsenetwork_pa_t_kernel(tc, x, W0, b0, m0, W1, b1, m1, out):
                 quantise_x(g + 2)
             if g + 1 < GROUPS:
                 regroup_h_on_vector(g + 1)
-            layer2(g)
-            relu_on_gpsimd(g)
+            new_results(g)
             if g + 2 < GROUPS:
-                layer1(g + 2)
+                new_h_lines(g + 2)
+            layer2_block(g, 0)
+            for i in range(PACK):
+                if i + 1 < PACK:
+                    layer2_block(g, i + 1)
+                if g + 2 < GROUPS:
+                    layer1_plane(g + 2, i)
+            relu_on_gpsimd(g)
             if g + 4 < GROUPS:
                 transpose_x(g + 4)
             if g + 2 < GROUPS:

@@ -18,8 +18,8 @@ TOKENS = 8192
 GROUPS = TOKENS // WIDTH
 HALF = WIDTH // 2
 LINE = 8
-SCALAR_TOKENS = {g: 128 for g in range(GROUPS)}
-SCALAR_TOKENS[GROUPS - 1] = 384
+SCALAR_TOKENS = {g: 112 for g in range(GROUPS)}
+SCALAR_TOKENS[GROUPS - 1] = 256
 SCALAR_TOKENS[0] = SCALAR_TOKENS[1] = 0
 FLOAT32_MAX = 3.4028234663852886e38
 
@@ -240,9 +240,10 @@ def tile_patchedsparsenetwork_pa_t_kernel(tc, x, W0, b0, m0, W1, b1, m1, out):
             relu_scalar(results[g][:, PACK - 1, :])
             nc.sync.dma_start(out=out_groups[g][:, PACK // 2 :, :], in_=results[g][:, PACK // 2 :, :])
 
-        def relu_and_store_block(g, r, relu):
-            relu(results[g][:, r, :])
-            nc.sync.dma_start(out=out_groups[g][:, r, :], in_=results[g][:, r, :])
+        def relu_and_store_blocks(g, relus):
+            for r, relu in enumerate(relus):
+                relu(results[g][:, r, :])
+                nc.sync.dma_start(out=out_groups[g][:, r, :], in_=results[g][:, r, :])
 
         b0_f32 = consts.tile([P, PACK], F32)
         transpose_x(0)
@@ -272,14 +273,16 @@ def tile_patchedsparsenetwork_pa_t_kernel(tc, x, W0, b0, m0, W1, b1, m1, out):
         transpose_x(4)
         new_h_grouped(2)
         regroup_h_on_scalar(2)
-        relu_on_scalar(0)
         last = GROUPS - 1
-        for g in range(1, last):
-            quantise_h(g)
+        for g in range(1, GROUPS):
+            if g < last:
+                quantise_h(g)
             if g + 2 < GROUPS:
                 quantise_x(g + 2)
             if g + 1 < GROUPS:
                 regroup_h_on_vector(g + 1)
+            if g == last - 1:
+                quantise_h(last)
             new_results(g)
             if g + 2 < GROUPS:
                 new_h_lines(g + 2)
@@ -289,16 +292,15 @@ def tile_patchedsparsenetwork_pa_t_kernel(tc, x, W0, b0, m0, W1, b1, m1, out):
                     layer2_block(g, i + 1)
                 if g + 2 < GROUPS:
                     layer1_plane(g + 2, i)
-            relu_on_gpsimd(g)
+            if g < last - 1:
+                relu_on_gpsimd(g)
             if g + 4 < GROUPS:
                 transpose_x(g + 4)
+            if g < last:
+                relu_on_scalar(g - 1)
             if g + 2 < GROUPS:
                 new_h_grouped(g + 2)
                 regroup_h_on_scalar(g + 2)
-            relu_on_scalar(g)
-        quantise_h(last)
-        layer2(last)
-        relu_and_store_block(last, 0, relu_gpsimd)
-        relu_and_store_block(last, 1, relu_scalar)
-        relu_and_store_block(last, 2, relu_scalar)
-        relu_and_store_block(last, 3, relu_vector)
+            if g == last - 1:
+                relu_and_store_blocks(g, (relu_gpsimd, relu_scalar, relu_gpsimd, relu_scalar))
+        relu_and_store_blocks(last, (relu_scalar, relu_gpsimd, relu_scalar, relu_vector))

from contextlib import ExitStack

import concourse.mybir as mybir
from concourse.masks import make_identity

F32 = mybir.dt.float32
BF16 = mybir.dt.bfloat16
U32 = mybir.dt.uint32
U8 = mybir.dt.uint8
FP8X4 = mybir.dt.float8_e4m3fn_x4
ALU = mybir.AluOpType
ACT = mybir.ActivationFunctionType

P = 128
PACK = 4
WIDTH = P * PACK
TOKENS = 8192
GROUPS = TOKENS // WIDTH
HALF = WIDTH // 2
LINE = 8
SCALAR_TOKENS = {g: 112 for g in range(GROUPS)}
SCALAR_TOKENS[GROUPS - 1] = 256
SCALAR_TOKENS[0] = SCALAR_TOKENS[1] = 0
FLOAT32_MAX = 3.4028234663852886e38

FLOPS = 2 * 2 * TOKENS * WIDTH * WIDTH


def tile_patchedsparsenetwork_pa_t_kernel(tc, x, W0, b0, m0, W1, b1, m1, out):
    nc = tc.nc
    x_groups = x.rearrange("(g p r) k -> g p (r k)", p=P, r=PACK)
    out_groups = out.rearrange("(g p r) d -> g p r d", p=P, r=PACK)

    with ExitStack() as ctx:
        consts = ctx.enter_context(tc.tile_pool(name="consts", bufs=1))
        x_pool = ctx.enter_context(tc.tile_pool(name="x_pool", bufs=GROUPS))
        grouped_pool = ctx.enter_context(tc.tile_pool(name="grouped_pool", bufs=3))
        mx_pool = ctx.enter_context(tc.tile_pool(name="mx_pool", bufs=3))
        out_pool = ctx.enter_context(tc.tile_pool(name="out_pool", bufs=4))
        psum_scalar = ctx.enter_context(tc.psum_pool(name="psum_scalar", bufs=4))
        psum_vector = ctx.enter_context(tc.psum_pool(name="psum_vector", bufs=4))
        ctx.enter_context(tc.manual_schedule())

        x_rows = {}

        def load_x(g):
            x_rows[g] = x_pool.tile([P, PACK * WIDTH], BF16, name="x_rows", tag="x_rows")
            pieces = 2 if g == 0 else 1
            for piece in range(pieces):
                cols = slice(piece * PACK * WIDTH // pieces, (piece + 1) * PACK * WIDTH // pieces)
                nc.sync.dma_start(out=x_rows[g][:, cols], in_=x_groups[g][:, cols])

        def load_weight_and_mask(W, m, rows_of_partition, name):
            raw = consts.tile([P, PACK * WIDTH], BF16, name=name + "_raw")
            mask = consts.tile([P, PACK * WIDTH], BF16, name=name + "_mask")
            for half in range(2):
                for tile_, source in ((raw, W), (mask, m)):
                    nc.sync.dma_start(
                        out=tile_[:, half * PACK * HALF : (half + 1) * PACK * HALF].rearrange(
                            "m (b k) -> m b k", k=WIDTH
                        ),
                        in_=source.rearrange(rows_of_partition, m=P)[:, half * PACK // 2 : (half + 1) * PACK // 2, :],
                    )
            return raw, mask

        b0_bf = consts.tile([P, PACK], BF16)
        b1_bf = consts.tile([P, WIDTH], BF16)

        load_x(0)
        w0_raw, m0_raw = load_weight_and_mask(W0, m0, "(m t) k -> m t k", "w0")
        load_x(1)
        nc.sync.dma_start(out=b0_bf[:], in_=b0.rearrange("(m t) -> m t", t=PACK))
        w1_raw, m1_raw = load_weight_and_mask(W1, m1, "(j m) k -> m j k", "w1")
        load_x(2)
        nc.sync.dma_start(out=b1_bf[:], in_=b1.partition_broadcast(P))
        for g in range(3, GROUPS):
            load_x(g)

        ident = consts.tile([P, P], F32)
        make_identity(nc, ident[:])

        def rows_onto_partitions(words, grouped, copies=(nc.scalar.copy, nc.scalar.copy)):
            grouped_words = grouped[:].bitcast(F32).rearrange("q (c u) -> q c u", u=2)
            for half in range(2):
                bank = psum_scalar.tile([P, 2, HALF], F32, name="bank", tag="bank")
                for b in range(2):
                    for u in range(2):
                        nc.tensor.transpose(bank[:, u, b * P : (b + 1) * P], words[:, 2 * half + b, u, :], ident[:])
                copies[half](
                    out=grouped_words[:, half * HALF : (half + 1) * HALF, :], in_=bank[:].rearrange("q u c -> q c u")
                )

        def quantise_halves(grouped, codes, scales):
            for half in range(2):
                nc.vector.quantize_mx(
                    out=codes[:, half * HALF : (half + 1) * HALF].bitcast(FP8X4),
                    scales=scales[:, half * HALF : (half + 1) * HALF],
                    in_=grouped[:, half * PACK * HALF : (half + 1) * PACK * HALF],
                )

        def mask_weight(raw, mask, name):
            masked = consts.tile([P, PACK * WIDTH], BF16, name=name + "_masked")
            for b in range(PACK):
                cols = slice(b * WIDTH, (b + 1) * WIDTH)
                nc.vector.tensor_tensor(
                    out=masked[:, cols].rearrange("m (u q e) -> m u q e", u=2, e=2),
                    in0=raw[:, cols].rearrange("m (q u e) -> m u q e", u=2, e=2),
                    in1=mask[:, cols].rearrange("m (q u e) -> m u q e", u=2, e=2),
                    op=ALU.mult,
                )
            return masked

        def transpose_weight(masked, name):
            grouped = consts.tile([P, PACK * WIDTH], BF16, name=name + "_grouped", align_bytes=64)
            rows_onto_partitions(masked[:].bitcast(F32).rearrange("m (b u q) -> m b u q", b=PACK, u=2), grouped)
            return grouped

        def quantise_weight(grouped, name):
            codes = consts.tile([P, WIDTH], U32, name=name + "_codes", align_bytes=64)
            scales = consts.tile([P, WIDTH], U8, name=name + "_scales", align_bytes=64)
            quantise_halves(grouped, codes, scales)
            return codes, scales

        def mx_tiles(name):
            codes = mx_pool.tile([P, WIDTH], U32, name=name + "_codes", tag=name + "_codes", align_bytes=64)
            scales = mx_pool.tile([P, WIDTH], U8, name=name + "_scales", tag=name + "_scales", align_bytes=64)
            return codes, scales

        x_grouped = {}
        x_mx = {}
        h_lines = {}
        h_grouped = {}
        h_mx = {}
        results = {}

        def transpose_x(g, copies=(nc.scalar.copy, nc.scalar.copy)):
            x_grouped[g] = grouped_pool.tile(
                [P, PACK * WIDTH], BF16, name="x_grouped", tag="x_grouped", align_bytes=64
            )
            rows_onto_partitions(
                x_rows[g][:].bitcast(F32).rearrange("p (b q u) -> p b u q", b=PACK, u=2), x_grouped[g], copies
            )

        def quantise_x(g):
            x_mx[g] = mx_tiles("x")
            codes, scales = x_mx[g]
            nc.vector.quantize_mx(out=codes[:].bitcast(FP8X4), scales=scales[:], in_=x_grouped[g][:])

        def layer1(g):
            new_h_lines(g)
            for t in range(PACK):
                layer1_plane(g, t)

        def new_h_lines(g):
            h_lines[g] = grouped_pool.tile([P, PACK * WIDTH], BF16, name="h_lines", tag="h_lines", align_bytes=64)

        def layer1_plane(g, t):
            codes, scales = x_mx[g]
            acc = psum_scalar.tile([P, WIDTH], F32, name="acc1", tag="bank")
            nc.tensor.matmul_mx(
                out=acc[:],
                lhsT=w0_codes[:, t * P : (t + 1) * P].bitcast(FP8X4),
                lhsT_scale=w0_scales[:, t * P : (t + 1) * P],
                rhs=codes[:].bitcast(FP8X4),
                rhs_scale=scales[:],
                start=True,
                stop=True,
            )
            nc.scalar.activation(
                out=h_lines[g][:].rearrange("p (c t i) -> p c t i", i=LINE, t=PACK)[:, :, t, :],
                in_=acc[:].rearrange("p (c i) -> p c i", i=LINE),
                func=ACT.Relu,
                bias=b0_f32[:, t : t + 1],
                scale=1.0,
            )

        def regroup_views(g, tokens):
            elements = slice(tokens.start * PACK, tokens.stop * PACK)
            return (
                h_grouped[g][:, elements].rearrange("p (c i t) -> p c t i", i=LINE, t=PACK),
                h_lines[g][:, elements].rearrange("p (c t i) -> p c t i", i=LINE, t=PACK),
            )

        def new_h_grouped(g):
            h_grouped[g] = grouped_pool.tile(
                [P, PACK * WIDTH], BF16, name="h_grouped", tag="h_grouped", align_bytes=64
            )

        def regroup_h_on_scalar(g):
            grouped, planes = regroup_views(g, slice(WIDTH - SCALAR_TOKENS[g], WIDTH))
            nc.scalar.copy(out=grouped, in_=planes)

        def regroup_h_on_vector(g):
            grouped, planes = regroup_views(g, slice(0, WIDTH - SCALAR_TOKENS[g]))
            nc.vector.tensor_copy(out=grouped, in_=planes)

        def quantise_h(g):
            h_mx[g] = mx_tiles("h")
            quantise_halves(h_grouped[g], h_mx[g][0], h_mx[g][1])

        def layer2(g):
            new_results(g)
            for r in range(PACK):
                layer2_block(g, r)

        def new_results(g):
            results[g] = out_pool.tile([P, PACK, WIDTH], F32, name="result", tag="result")

        def layer2_block(g, r):
            codes, scales = h_mx[g]
            acc = psum_vector.tile([P, WIDTH], F32, name="acc2", tag="acc2")
            nc.tensor.matmul_mx(
                out=acc[:],
                lhsT=codes[:, r * P : (r + 1) * P].bitcast(FP8X4),
                lhsT_scale=scales[:, r * P : (r + 1) * P],
                rhs=w1_codes[:].bitcast(FP8X4),
                rhs_scale=w1_scales[:],
                start=True,
                stop=True,
            )
            nc.vector.tensor_tensor(out=results[g][:, r, :], in0=acc[:], in1=b1_bf[:], op=ALU.add)

        def relu_gpsimd(block):
            nc.gpsimd.tensor_scalar(
                out=block, in0=block, scalar1=FLOAT32_MAX, scalar2=0.0, op0=ALU.min, op1=ALU.max
            )

        def relu_scalar(block):
            nc.scalar.activation(out=block, in_=block, func=ACT.Relu)

        def relu_vector(block):
            nc.vector.tensor_scalar(out=block, in0=block, scalar1=0.0, scalar2=None, op0=ALU.max)

        def relu_on_gpsimd(g):
            for r in range(PACK - 1):
                relu_gpsimd(results[g][:, r, :])
            nc.sync.dma_start(out=out_groups[g][:, : PACK // 2, :], in_=results[g][:, : PACK // 2, :])

        def relu_on_scalar(g):
            relu_scalar(results[g][:, PACK - 1, :])
            nc.sync.dma_start(out=out_groups[g][:, PACK // 2 :, :], in_=results[g][:, PACK // 2 :, :])

        def relu_and_store_blocks(g, relus):
            for r, relu in enumerate(relus):
                relu(results[g][:, r, :])
                nc.sync.dma_start(out=out_groups[g][:, r, :], in_=results[g][:, r, :])

        b0_f32 = consts.tile([P, PACK], F32)
        transpose_x(0)
        w0_masked = mask_weight(w0_raw, m0_raw, "w0")
        quantise_x(0)
        w0_grouped = transpose_weight(w0_masked, "w0")
        w0_codes, w0_scales = quantise_weight(w0_grouped, "w0")
        transpose_x(1, (nc.scalar.copy, nc.vector.tensor_copy))
        nc.scalar.copy(out=b0_f32[:], in_=b0_bf[:])
        layer1(0)
        w1_masked = mask_weight(w1_raw, m1_raw, "w1")
        quantise_x(1)
        w1_grouped = transpose_weight(w1_masked, "w1")
        transpose_x(2)
        new_h_grouped(0)
        regroup_h_on_vector(0)
        layer1(1)
        w1_codes, w1_scales = quantise_weight(w1_grouped, "w1")
        quantise_h(0)
        quantise_x(2)
        layer2(0)
        relu_on_gpsimd(0)
        new_h_grouped(1)
        regroup_h_on_vector(1)
        transpose_x(3)
        layer1(2)
        transpose_x(4)
        new_h_grouped(2)
        regroup_h_on_scalar(2)
        last = GROUPS - 1
        for g in range(1, GROUPS):
            if g < last:
                quantise_h(g)
            if g + 2 < GROUPS:
                quantise_x(g + 2)
            if g + 1 < GROUPS:
                regroup_h_on_vector(g + 1)
            if g == last - 1:
                quantise_h(last)
            new_results(g)
            if g + 2 < GROUPS:
                new_h_lines(g + 2)
            layer2_block(g, 0)
            for i in range(PACK):
                if i + 1 < PACK:
                    layer2_block(g, i + 1)
                if g + 2 < GROUPS:
                    layer1_plane(g + 2, i)
            if g < last - 1:
                relu_on_gpsimd(g)
            if g + 4 < GROUPS:
                transpose_x(g + 4)
            if g < last:
                relu_on_scalar(g - 1)
            if g + 2 < GROUPS:
                new_h_grouped(g + 2)
                regroup_h_on_scalar(g + 2)
            if g == last - 1:
                relu_and_store_blocks(g, (relu_gpsimd, relu_scalar, relu_gpsimd, relu_scalar))
        relu_and_store_blocks(last, (relu_scalar, relu_gpsimd, relu_scalar, relu_vector))
